import numpy as np
import ml_dtypes

BF16 = ml_dtypes.bfloat16


def bf(x):
    return np.asarray(x, np.float32).astype(BF16)


def f32(x):
    return np.asarray(x, np.float32)


def f64(x):
    return np.asarray(x).astype(np.float64)


def striped(idx):
    return np.tile(idx.reshape(-1, 16).T, (8, 1))


C, F, F2, S, N = 256, 256, 512, 1024, 128
EPS = 1e-6


def silu(v):
    return v / (1.0 + np.exp(-v))


def setup_inputs():
    return {"base": f32(np.random.standard_normal((C, S))), "x": f32(np.random.standard_normal((C, N))), "ln_s": f32(1.0 + 0.1 * np.random.standard_normal((C, 1))), "ln_b": f32(0.1 * np.random.standard_normal((C, 1))), "w1": bf(np.random.standard_normal((C, F2)) / np.sqrt(C)), "w2": bf(2.0 * np.random.standard_normal((F, C)) / np.sqrt(F)), "ls": f32(0.5 * (1.0 + 0.2 * np.random.standard_normal((C, 1)))), "offs": striped(np.random.permutation(S)[:N])}


def reference(base, x, ln_s, ln_b, w1, w2, ls, offs):
    idx = offs[:16].T.reshape(-1)
    xx = f64(x)
    mu = xx.mean(0, keepdims=True)
    var = ((xx - mu) ** 2).mean(0, keepdims=True)
    h = (xx - mu) / np.sqrt(var + EPS) * f64(ln_s) + f64(ln_b)
    p = f64(w1).T @ h
    u = silu(p[:F]) * p[F:]
    t = f64(ls) * (f64(w2).T @ u)
    out = f64(base).copy()
    out[:, idx] = xx + t
    return out

@@ -1,0 +1,102 @@
+import concourse.mybir as mybir
+
+F32 = mybir.dt.float32
+BF16 = mybir.dt.bfloat16
+U16 = mybir.dt.uint16
+ALU = mybir.AluOpType
+ACT = mybir.ActivationFunctionType
+
+P = 128
+C, F, S, N = 256, 256, 1024, 128
+CB = C // P
+FB = F // P
+EPS = 1e-6
+FLOPS = 2 * N * (C * 2 * F + F * C)
+
+
+def tile_lunarismind_kernel(tc, base, x, ln_s, ln_b, w1, w2, ls, offs, out):
+    nc = tc.nc
+    x_blocks = x.rearrange("(k p) j -> k p j", p=P)
+    base_blocks = base.rearrange("(k p) s -> k p s", p=P)
+    out_blocks = out.rearrange("(k p) s -> k p s", p=P)
+
+    with (
+        tc.tile_pool(name="held", bufs=1) as held,
+        tc.tile_pool(name="work", bufs=2) as work,
+        tc.psum_pool(name="psum", bufs=1) as psum,
+    ):
+        x_sb = [held.tile([P, N], F32, name=f"x_sb{k}") for k in range(CB)]
+        nc.sync.dma_start(x_sb[0][:], x_blocks[0])
+        nc.scalar.dma_start(x_sb[1][:], x_blocks[1])
+
+        offsets = held.tile([P, N // 16], U16, name="offsets")
+        nc.sync.dma_start(offsets[:], offs)
+
+        w1_sb = held.tile([P, CB, 2 * F], BF16, name="w1_sb")
+        nc.scalar.dma_start(w1_sb[:], w1.rearrange("(k p) f -> p k f", p=P))
+        w2_sb = held.tile([P, FB, C], BF16, name="w2_sb")
+        nc.scalar.dma_start(w2_sb[:], w2.rearrange("(k p) c -> p k c", p=P))
+
+        gain = held.tile([P, CB], F32, name="gain")
+        shift = held.tile([P, CB], F32, name="shift")
+        layer_scale = held.tile([P, CB], F32, name="layer_scale")
+        with nc.allow_non_contiguous_dma(reason="256 floats, one to a partition and block"):
+            nc.sync.dma_start(gain[:], ln_s.rearrange("(k p) o -> p (k o)", p=P))
+            nc.sync.dma_start(shift[:], ln_b.rearrange("(k p) o -> p (k o)", p=P))
+            nc.scalar.dma_start(layer_scale[:], ls.rearrange("(k p) o -> p (k o)", p=P))
+
+        window = [held.tile([P, S], F32, name=f"window{k}") for k in range(CB)]
+        nc.sync.dma_start(window[0][:], base_blocks[0])
+        nc.scalar.dma_start(window[1][:], base_blocks[1])
+
+        averager = held.tile([P, P], F32, name="averager")
+        nc.gpsimd.memset(averager[:], 1.0 / C)
+        eps = held.tile([P, 1], F32, name="eps")
+        nc.gpsimd.memset(eps[:], EPS)
+
+        mean_ps = psum.tile([P, N], F32, name="mean_ps")
+        for k in range(CB):
+            nc.tensor.matmul(mean_ps[:], averager[:], x_sb[k][:], start=(k == 0), stop=(k == CB - 1))
+
+        centred = [held.tile([P, N], F32, name=f"centred{k}") for k in range(CB)]
+        var_ps = psum.tile([P, N], F32, name="var_ps")
+        for k in range(CB):
+            nc.vector.tensor_tensor(centred[k][:], x_sb[k][:], mean_ps[:], ALU.subtract)
+            squared = work.tile([P, N], F32, name="squared")
+            nc.scalar.activation(squared[:], centred[k][:], ACT.Square)
+            nc.tensor.matmul(var_ps[:], averager[:], squared[:], start=(k == 0), stop=(k == CB - 1))
+
+        rstd = held.tile([P, N], F32, name="rstd")
+        nc.scalar.activation(rstd[:], var_ps[:], ACT.Abs_reciprocal_sqrt, bias=eps[:])
+
+        h = [held.tile([P, N], BF16, name=f"h{k}") for k in range(CB)]
+        for k in range(CB):
+            normed = work.tile([P, N], F32, name="normed")
+            nc.vector.scalar_tensor_tensor(
+                normed[:], centred[k][:], gain[:, k : k + 1], rstd[:], ALU.mult, ALU.mult
+            )
+            nc.vector.tensor_scalar(h[k][:], normed[:], shift[:, k : k + 1], None, ALU.add)
+
+        u = [held.tile([P, N], BF16, name=f"u{fb}") for fb in range(FB)]
+        for fb in range(FB):
+            gate_ps = psum.tile([P, N], F32, name=f"gate_ps{fb}")
+            value_ps = psum.tile([P, N], F32, name=f"value_ps{fb}")
+            for product_ps, first in ((gate_ps, fb * P), (value_ps, F + fb * P)):
+                for k in range(CB):
+                    nc.tensor.matmul(
+                        product_ps[:], w1_sb[:, k, first : first + P], h[k][:], start=(k == 0), stop=(k == CB - 1)
+                    )
+            gated = work.tile([P, N], F32, name="gated")
+            nc.scalar.activation(gated[:], gate_ps[:], ACT.Silu)
+            nc.vector.tensor_tensor(u[fb][:], gated[:], value_ps[:], ALU.mult)
+
+        for k in range(CB):
+            branch_ps = psum.tile([P, N], F32, name=f"branch_ps{k}")
+            for fb in range(FB):
+                nc.tensor.matmul(
+                    branch_ps[:], w2_sb[:, fb, k * P : (k + 1) * P], u[fb][:], start=(fb == 0), stop=(fb == FB - 1)
+                )
+            t = work.tile([P, N], F32, name="t")
+            nc.scalar.activation(t[:], branch_ps[:], ACT.Identity, scale=layer_scale[:, k : k + 1])
+            nc.vector.tensor_tensor(window[k][:].indirect(offsets[:]), x_sb[k][:], t[:], ALU.add)
+            nc.sync.dma_start(out_blocks[k], window[k][:])

@@ -29,11 +29,8 @@ def tile_lunarismind_kernel(tc, base, x, ln_s, ln_b, w1, w2, ls, offs, out):
         nc.sync.dma_start(x_sb[0][:], x_blocks[0])
         nc.scalar.dma_start(x_sb[1][:], x_blocks[1])
 
-        offsets = held.tile([P, N // 16], U16, name="offsets")
-        nc.sync.dma_start(offsets[:], offs)
-
         w1_sb = held.tile([P, CB, 2 * F], BF16, name="w1_sb")
-        nc.scalar.dma_start(w1_sb[:], w1.rearrange("(k p) f -> p k f", p=P))
+        nc.sync.dma_start(w1_sb[:], w1.rearrange("(k p) f -> p k f", p=P))
         w2_sb = held.tile([P, FB, C], BF16, name="w2_sb")
         nc.scalar.dma_start(w2_sb[:], w2.rearrange("(k p) c -> p k c", p=P))
 
@@ -45,14 +42,20 @@ def tile_lunarismind_kernel(tc, base, x, ln_s, ln_b, w1, w2, ls, offs, out):
             nc.sync.dma_start(shift[:], ln_b.rearrange("(k p) o -> p (k o)", p=P))
             nc.scalar.dma_start(layer_scale[:], ls.rearrange("(k p) o -> p (k o)", p=P))
 
+        offsets = held.tile([P, N // 16], U16, name="offsets")
+        nc.sync.dma_start(offsets[:], offs)
+
         window = [held.tile([P, S], F32, name=f"window{k}") for k in range(CB)]
         nc.sync.dma_start(window[0][:], base_blocks[0])
         nc.scalar.dma_start(window[1][:], base_blocks[1])
 
         averager = held.tile([P, P], F32, name="averager")
-        nc.gpsimd.memset(averager[:], 1.0 / C)
+        nc.vector.memset(averager[:], 1.0 / C)
         eps = held.tile([P, 1], F32, name="eps")
-        nc.gpsimd.memset(eps[:], EPS)
+        nc.vector.memset(eps[:], EPS)
+
+        table_warmer = held.tile([P, 2], F32, name="table_warmer")
+        nc.scalar.activation(table_warmer[:, 0:1], eps[:], ACT.Abs_reciprocal_sqrt)
 
         mean_ps = psum.tile([P, N], F32, name="mean_ps")
         for k in range(CB):
@@ -63,11 +66,12 @@ def tile_lunarismind_kernel(tc, base, x, ln_s, ln_b, w1, w2, ls, offs, out):
         for k in range(CB):
             nc.vector.tensor_tensor(centred[k][:], x_sb[k][:], mean_ps[:], ALU.subtract)
             squared = work.tile([P, N], F32, name="squared")
-            nc.scalar.activation(squared[:], centred[k][:], ACT.Square)
+            nc.vector.tensor_tensor(squared[:], centred[k][:], centred[k][:], ALU.mult)
             nc.tensor.matmul(var_ps[:], averager[:], squared[:], start=(k == 0), stop=(k == CB - 1))
 
         rstd = held.tile([P, N], F32, name="rstd")
         nc.scalar.activation(rstd[:], var_ps[:], ACT.Abs_reciprocal_sqrt, bias=eps[:])
+        nc.scalar.activation(table_warmer[:, 1:2], rstd[:, 0:1], ACT.Silu)
 
         h = [held.tile([P, N], BF16, name=f"h{k}") for k in range(CB)]
         for k in range(CB):
@@ -77,26 +81,26 @@ def tile_lunarismind_kernel(tc, base, x, ln_s, ln_b, w1, w2, ls, offs, out):
             )
             nc.vector.tensor_scalar(h[k][:], normed[:], shift[:, k : k + 1], None, ALU.add)
 
+        p_ps = [psum.tile([P, N], F32, name=f"p_ps{q}") for q in range(2 * FB)]
+        for k in range(CB):
+            for q in range(2 * FB):
+                nc.tensor.matmul(
+                    p_ps[q][:], w1_sb[:, k, q * P : (q + 1) * P], h[k][:], start=(k == 0), stop=(k == CB - 1)
+                )
         u = [held.tile([P, N], BF16, name=f"u{fb}") for fb in range(FB)]
         for fb in range(FB):
-            gate_ps = psum.tile([P, N], F32, name=f"gate_ps{fb}")
-            value_ps = psum.tile([P, N], F32, name=f"value_ps{fb}")
-            for product_ps, first in ((gate_ps, fb * P), (value_ps, F + fb * P)):
-                for k in range(CB):
-                    nc.tensor.matmul(
-                        product_ps[:], w1_sb[:, k, first : first + P], h[k][:], start=(k == 0), stop=(k == CB - 1)
-                    )
             gated = work.tile([P, N], F32, name="gated")
-            nc.scalar.activation(gated[:], gate_ps[:], ACT.Silu)
-            nc.vector.tensor_tensor(u[fb][:], gated[:], value_ps[:], ALU.mult)
+            nc.scalar.activation(gated[:], p_ps[fb][:], ACT.Silu)
+            nc.vector.tensor_tensor(u[fb][:], gated[:], p_ps[FB + fb][:], ALU.mult)
 
-        for k in range(CB):
-            branch_ps = psum.tile([P, N], F32, name=f"branch_ps{k}")
-            for fb in range(FB):
+        branch_ps = [psum.tile([P, N], F32, name=f"branch_ps{k}") for k in range(CB)]
+        for fb in range(FB):
+            for k in range(CB):
                 nc.tensor.matmul(
-                    branch_ps[:], w2_sb[:, fb, k * P : (k + 1) * P], u[fb][:], start=(fb == 0), stop=(fb == FB - 1)
+                    branch_ps[k][:], w2_sb[:, fb, k * P : (k + 1) * P], u[fb][:], start=(fb == 0), stop=(fb == FB - 1)
                 )
+        for k in range(CB):
             t = work.tile([P, N], F32, name="t")
-            nc.scalar.activation(t[:], branch_ps[:], ACT.Identity, scale=layer_scale[:, k : k + 1])
+            nc.scalar.activation(t[:], branch_ps[k][:], ACT.Identity, scale=layer_scale[:, k : k + 1])
             nc.vector.tensor_tensor(window[k][:].indirect(offsets[:]), x_sb[k][:], t[:], ALU.add)
-            nc.sync.dma_start(out_blocks[k], window[k][:])
+            (nc.sync, nc.scalar)[k].dma_start(out_blocks[k], window[k][:])

@@ -12,6 +12,7 @@ CB = C // P
 FB = F // P
 EPS = 1e-6
 FLOPS = 2 * N * (C * 2 * F + F * C)
+WARM_UP_MATMULS = 4
 
 
 def tile_lunarismind_kernel(tc, base, x, ln_s, ln_b, w1, w2, ls, offs, out):
@@ -58,11 +59,15 @@ def tile_lunarismind_kernel(tc, base, x, ln_s, ln_b, w1, w2, ls, offs, out):
         nc.scalar.activation(table_warmer[:, 0:1], eps[:], ACT.Abs_reciprocal_sqrt)
 
         mean_ps = psum.tile([P, N], F32, name="mean_ps")
+        var_ps = psum.tile([P, N], F32, name="var_ps")
+
+        for repeat in range(WARM_UP_MATMULS):
+            nc.tensor.matmul(var_ps[:], averager[:], averager[:], start=True, stop=True)
+
         for k in range(CB):
             nc.tensor.matmul(mean_ps[:], averager[:], x_sb[k][:], start=(k == 0), stop=(k == CB - 1))
 
         centred = [held.tile([P, N], F32, name=f"centred{k}") for k in range(CB)]
-        var_ps = psum.tile([P, N], F32, name="var_ps")
         for k in range(CB):
             nc.vector.tensor_tensor(centred[k][:], x_sb[k][:], mean_ps[:], ALU.subtract)
             squared = work.tile([P, N], F32, name="squared")

@@ -12,7 +12,13 @@ CB = C // P
 FB = F // P
 EPS = 1e-6
 FLOPS = 2 * N * (C * 2 * F + F * C)
-WARM_UP_MATMULS = 4
+WARM_UP_MATMULS = 3
+FILL_MATMULS = 2
+
+
+def spin(nc, idle_ps, averager, moving, count):
+    for repeat in range(count):
+        nc.tensor.matmul(idle_ps[:], averager[:], moving[:], start=True, stop=True)
 
 
 def tile_lunarismind_kernel(tc, base, x, ln_s, ln_b, w1, w2, ls, offs, out):
@@ -61,11 +67,14 @@ def tile_lunarismind_kernel(tc, base, x, ln_s, ln_b, w1, w2, ls, offs, out):
         mean_ps = psum.tile([P, N], F32, name="mean_ps")
         var_ps = psum.tile([P, N], F32, name="var_ps")
 
-        for repeat in range(WARM_UP_MATMULS):
-            nc.tensor.matmul(var_ps[:], averager[:], averager[:], start=True, stop=True)
+        branch_ps = [psum.tile([P, N], F32, name=f"branch_ps{k}") for k in range(CB)]
+        idle_ps = branch_ps[CB - 1]
+
+        spin(nc, idle_ps, averager, averager, WARM_UP_MATMULS)
 
         for k in range(CB):
             nc.tensor.matmul(mean_ps[:], averager[:], x_sb[k][:], start=(k == 0), stop=(k == CB - 1))
+        spin(nc, idle_ps, averager, x_sb[CB - 1], FILL_MATMULS)
 
         centred = [held.tile([P, N], F32, name=f"centred{k}") for k in range(CB)]
         for k in range(CB):
@@ -73,6 +82,7 @@ def tile_lunarismind_kernel(tc, base, x, ln_s, ln_b, w1, w2, ls, offs, out):
             squared = work.tile([P, N], F32, name="squared")
             nc.vector.tensor_tensor(squared[:], centred[k][:], centred[k][:], ALU.mult)
             nc.tensor.matmul(var_ps[:], averager[:], squared[:], start=(k == 0), stop=(k == CB - 1))
+        spin(nc, idle_ps, averager, squared, FILL_MATMULS)
 
         rstd = held.tile([P, N], F32, name="rstd")
         nc.scalar.activation(rstd[:], var_ps[:], ACT.Abs_reciprocal_sqrt, bias=eps[:])
@@ -98,7 +108,6 @@ def tile_lunarismind_kernel(tc, base, x, ln_s, ln_b, w1, w2, ls, offs, out):
             nc.scalar.activation(gated[:], p_ps[fb][:], ACT.Silu)
             nc.vector.tensor_tensor(u[fb][:], gated[:], p_ps[FB + fb][:], ALU.mult)
 
-        branch_ps = [psum.tile([P, N], F32, name=f"branch_ps{k}") for k in range(CB)]
         for fb in range(FB):
             for k in range(CB):
                 nc.tensor.matmul(

@@ -117,4 +117,6 @@ def tile_lunarismind_kernel(tc, base, x, ln_s, ln_b, w1, w2, ls, offs, out):
             t = work.tile([P, N], F32, name="t")
             nc.scalar.activation(t[:], branch_ps[k][:], ACT.Identity, scale=layer_scale[:, k : k + 1])
             nc.vector.tensor_tensor(window[k][:].indirect(offsets[:]), x_sb[k][:], t[:], ALU.add)
-            (nc.sync, nc.scalar)[k].dma_start(out_blocks[k], window[k][:])
+            for half, queue in enumerate((nc.sync, nc.scalar)):
+                columns = slice(half * (S // 2), (half + 1) * (S // 2))
+                queue.dma_start(out_blocks[k][:, columns], window[k][:, columns])

@@ -34,12 +34,10 @@ def tile_lunarismind_kernel(tc, base, x, ln_s, ln_b, w1, w2, ls, offs, out):
     ):
         x_sb = [held.tile([P, N], F32, name=f"x_sb{k}") for k in range(CB)]
         nc.sync.dma_start(x_sb[0][:], x_blocks[0])
-        nc.scalar.dma_start(x_sb[1][:], x_blocks[1])
+        nc.sync.dma_start(x_sb[1][:], x_blocks[1])
 
         w1_sb = held.tile([P, CB, 2 * F], BF16, name="w1_sb")
         nc.sync.dma_start(w1_sb[:], w1.rearrange("(k p) f -> p k f", p=P))
-        w2_sb = held.tile([P, FB, C], BF16, name="w2_sb")
-        nc.scalar.dma_start(w2_sb[:], w2.rearrange("(k p) c -> p k c", p=P))
 
         gain = held.tile([P, CB], F32, name="gain")
         shift = held.tile([P, CB], F32, name="shift")
@@ -47,22 +45,23 @@ def tile_lunarismind_kernel(tc, base, x, ln_s, ln_b, w1, w2, ls, offs, out):
         with nc.allow_non_contiguous_dma(reason="256 floats, one to a partition and block"):
             nc.sync.dma_start(gain[:], ln_s.rearrange("(k p) o -> p (k o)", p=P))
             nc.sync.dma_start(shift[:], ln_b.rearrange("(k p) o -> p (k o)", p=P))
-            nc.scalar.dma_start(layer_scale[:], ls.rearrange("(k p) o -> p (k o)", p=P))
+
+        w2_sb = held.tile([P, FB, C], BF16, name="w2_sb")
+        nc.sync.dma_start(w2_sb[:], w2.rearrange("(k p) c -> p k c", p=P))
+        with nc.allow_non_contiguous_dma(reason="256 floats, one to a partition and block"):
+            nc.sync.dma_start(layer_scale[:], ls.rearrange("(k p) o -> p (k o)", p=P))
 
         offsets = held.tile([P, N // 16], U16, name="offsets")
         nc.sync.dma_start(offsets[:], offs)
 
         window = [held.tile([P, S], F32, name=f"window{k}") for k in range(CB)]
-        nc.sync.dma_start(window[0][:], base_blocks[0])
-        nc.scalar.dma_start(window[1][:], base_blocks[1])
+        for k in range(CB):
+            nc.sync.dma_start(window[k][:], base_blocks[k])
 
         averager = held.tile([P, P], F32, name="averager")
         nc.vector.memset(averager[:], 1.0 / C)
         eps = held.tile([P, 1], F32, name="eps")
         nc.vector.memset(eps[:], EPS)
-
-        table_warmer = held.tile([P, 2], F32, name="table_warmer")
-        nc.scalar.activation(table_warmer[:, 0:1], eps[:], ACT.Abs_reciprocal_sqrt)
 
         mean_ps = psum.tile([P, N], F32, name="mean_ps")
         var_ps = psum.tile([P, N], F32, name="var_ps")
@@ -86,7 +85,6 @@ def tile_lunarismind_kernel(tc, base, x, ln_s, ln_b, w1, w2, ls, offs, out):
 
         rstd = held.tile([P, N], F32, name="rstd")
         nc.scalar.activation(rstd[:], var_ps[:], ACT.Abs_reciprocal_sqrt, bias=eps[:])
-        nc.scalar.activation(table_warmer[:, 1:2], rstd[:, 0:1], ACT.Silu)
 
         h = [held.tile([P, N], BF16, name=f"h{k}") for k in range(CB)]
         for k in range(CB):
@@ -113,10 +111,11 @@ def tile_lunarismind_kernel(tc, base, x, ln_s, ln_b, w1, w2, ls, offs, out):
                 nc.tensor.matmul(
                     branch_ps[k][:], w2_sb[:, fb, k * P : (k + 1) * P], u[fb][:], start=(fb == 0), stop=(fb == FB - 1)
                 )
+        t = [held.tile([P, N], F32, name=f"t{k}") for k in range(CB)]
+        nc.vector.tensor_scalar(t[0][:], branch_ps[0][:], layer_scale[:, 0:1], None, ALU.mult)
+        nc.scalar.activation(t[1][:], branch_ps[1][:], ACT.Identity, scale=layer_scale[:, 1:2])
         for k in range(CB):
-            t = work.tile([P, N], F32, name="t")
-            nc.scalar.activation(t[:], branch_ps[k][:], ACT.Identity, scale=layer_scale[:, k : k + 1])
-            nc.vector.tensor_tensor(window[k][:].indirect(offsets[:]), x_sb[k][:], t[:], ALU.add)
+            nc.vector.tensor_tensor(window[k][:].indirect(offsets[:]), x_sb[k][:], t[k][:], ALU.add)
             for half, queue in enumerate((nc.sync, nc.scalar)):
                 columns = slice(half * (S // 2), (half + 1) * (S // 2))
                 queue.dma_start(out_blocks[k][:, columns], window[k][:, columns])

@@ -1,4 +1,5 @@
 import concourse.mybir as mybir
+from concourse.masks import make_identity
 
 F32 = mybir.dt.float32
 BF16 = mybir.dt.bfloat16
@@ -12,13 +13,6 @@ CB = C // P
 FB = F // P
 EPS = 1e-6
 FLOPS = 2 * N * (C * 2 * F + F * C)
-WARM_UP_MATMULS = 3
-FILL_MATMULS = 2
-
-
-def spin(nc, idle_ps, averager, moving, count):
-    for repeat in range(count):
-        nc.tensor.matmul(idle_ps[:], averager[:], moving[:], start=True, stop=True)
 
 
 def tile_lunarismind_kernel(tc, base, x, ln_s, ln_b, w1, w2, ls, offs, out):
@@ -58,41 +52,28 @@ def tile_lunarismind_kernel(tc, base, x, ln_s, ln_b, w1, w2, ls, offs, out):
         for k in range(CB):
             nc.sync.dma_start(window[k][:], base_blocks[k])
 
-        averager = held.tile([P, P], F32, name="averager")
-        nc.vector.memset(averager[:], 1.0 / C)
+        identity = held.tile([P, P], F32, name="identity")
+        make_identity(nc, identity[:])
         eps = held.tile([P, 1], F32, name="eps")
         nc.vector.memset(eps[:], EPS)
 
-        mean_ps = psum.tile([P, N], F32, name="mean_ps")
-        var_ps = psum.tile([P, N], F32, name="var_ps")
-
-        branch_ps = [psum.tile([P, N], F32, name=f"branch_ps{k}") for k in range(CB)]
-        idle_ps = branch_ps[CB - 1]
-
-        spin(nc, idle_ps, averager, averager, WARM_UP_MATMULS)
-
+        x_t_ps = psum.tile([P, C], F32, name="x_t_ps")
         for k in range(CB):
-            nc.tensor.matmul(mean_ps[:], averager[:], x_sb[k][:], start=(k == 0), stop=(k == CB - 1))
-        spin(nc, idle_ps, averager, x_sb[CB - 1], FILL_MATMULS)
-
-        centred = [held.tile([P, N], F32, name=f"centred{k}") for k in range(CB)]
-        for k in range(CB):
-            nc.vector.tensor_tensor(centred[k][:], x_sb[k][:], mean_ps[:], ALU.subtract)
-            squared = work.tile([P, N], F32, name="squared")
-            nc.vector.tensor_tensor(squared[:], centred[k][:], centred[k][:], ALU.mult)
-            nc.tensor.matmul(var_ps[:], averager[:], squared[:], start=(k == 0), stop=(k == CB - 1))
-        spin(nc, idle_ps, averager, squared, FILL_MATMULS)
-
-        rstd = held.tile([P, N], F32, name="rstd")
-        nc.scalar.activation(rstd[:], var_ps[:], ACT.Abs_reciprocal_sqrt, bias=eps[:])
+            nc.tensor.transpose(x_t_ps[:, k * P : (k + 1) * P], x_sb[k][:], identity[:])
+        stats = held.tile([P, 6], F32, name="stats")
+        nc.vector.bn_stats(stats[:], x_t_ps[:])
+        mean_var = held.tile([P, 2], F32, name="mean_var")
+        nc.vector.bn_aggr(mean_var[:], stats[:])
+        rstd = held.tile([P, 1], F32, name="rstd")
+        nc.scalar.activation(rstd[:], mean_var[:, 1:2], ACT.Abs_reciprocal_sqrt, bias=eps[:])
+        normed_t = held.tile([P, C], F32, name="normed_t")
+        nc.vector.tensor_scalar(normed_t[:], x_t_ps[:], mean_var[:, 0:1], rstd[:], ALU.subtract, ALU.mult)
 
         h = [held.tile([P, N], BF16, name=f"h{k}") for k in range(CB)]
         for k in range(CB):
-            normed = work.tile([P, N], F32, name="normed")
-            nc.vector.scalar_tensor_tensor(
-                normed[:], centred[k][:], gain[:, k : k + 1], rstd[:], ALU.mult, ALU.mult
-            )
-            nc.vector.tensor_scalar(h[k][:], normed[:], shift[:, k : k + 1], None, ALU.add)
+            normed_ps = psum.tile([P, N], F32, name=f"normed_ps{k}", tag=f"channels{k}")
+            nc.tensor.transpose(normed_ps[:], normed_t[:, k * P : (k + 1) * P], identity[:])
+            nc.vector.tensor_scalar(h[k][:], normed_ps[:], gain[:, k : k + 1], shift[:, k : k + 1], ALU.mult, ALU.add)
 
         p_ps = [psum.tile([P, N], F32, name=f"p_ps{q}") for q in range(2 * FB)]
         for k in range(CB):
@@ -106,6 +87,7 @@ def tile_lunarismind_kernel(tc, base, x, ln_s, ln_b, w1, w2, ls, offs, out):
             nc.scalar.activation(gated[:], p_ps[fb][:], ACT.Silu)
             nc.vector.tensor_tensor(u[fb][:], gated[:], p_ps[FB + fb][:], ALU.mult)
 
+        branch_ps = [psum.tile([P, N], F32, name=f"branch_ps{k}", tag=f"channels{k}") for k in range(CB)]
         for fb in range(FB):
             for k in range(CB):
                 nc.tensor.matmul(

@@ -13,6 +13,13 @@ CB = C // P
 FB = F // P
 EPS = 1e-6
 FLOPS = 2 * N * (C * 2 * F + F * C)
+WARM_UP_MATMULS = 2
+FILL_MATMULS = 3
+
+
+def spin(nc, idle_ps, identity, moving, count):
+    for repeat in range(count):
+        nc.tensor.matmul(idle_ps[:], identity[:], moving[:], start=True, stop=True)
 
 
 def tile_lunarismind_kernel(tc, base, x, ln_s, ln_b, w1, w2, ls, offs, out):
@@ -57,9 +64,12 @@ def tile_lunarismind_kernel(tc, base, x, ln_s, ln_b, w1, w2, ls, offs, out):
         eps = held.tile([P, 1], F32, name="eps")
         nc.vector.memset(eps[:], EPS)
 
+        idle_ps = psum.tile([P, N], F32, name="idle_ps")
+        spin(nc, idle_ps, identity, identity, WARM_UP_MATMULS)
         x_t_ps = psum.tile([P, C], F32, name="x_t_ps")
         for k in range(CB):
             nc.tensor.transpose(x_t_ps[:, k * P : (k + 1) * P], x_sb[k][:], identity[:])
+        spin(nc, idle_ps, identity, x_sb[CB - 1], FILL_MATMULS)
         stats = held.tile([P, 6], F32, name="stats")
         nc.vector.bn_stats(stats[:], x_t_ps[:])
         mean_var = held.tile([P, 2], F32, name="mean_var")

@@ -64,25 +64,25 @@ def tile_lunarismind_kernel(tc, base, x, ln_s, ln_b, w1, w2, ls, offs, out):
         eps = held.tile([P, 1], F32, name="eps")
         nc.vector.memset(eps[:], EPS)
 
-        idle_ps = psum.tile([P, N], F32, name="idle_ps")
+        idle_ps = psum.tile([P, N], F32, name="idle_ps", tag="p_ps3")
         spin(nc, idle_ps, identity, identity, WARM_UP_MATMULS)
-        x_t_ps = psum.tile([P, C], F32, name="x_t_ps")
+        x_t_ps = [psum.tile([P, P], F32, name=f"x_t_ps{k}") for k in range(CB)]
+        stats = held.tile([P, CB, 6], F32, name="stats")
         for k in range(CB):
-            nc.tensor.transpose(x_t_ps[:, k * P : (k + 1) * P], x_sb[k][:], identity[:])
+            nc.tensor.transpose(x_t_ps[k][:], x_sb[k][:], identity[:])
+            nc.vector.bn_stats(stats[:, k, :], x_t_ps[k][:])
         spin(nc, idle_ps, identity, x_sb[CB - 1], FILL_MATMULS)
-        stats = held.tile([P, 6], F32, name="stats")
-        nc.vector.bn_stats(stats[:], x_t_ps[:])
         mean_var = held.tile([P, 2], F32, name="mean_var")
-        nc.vector.bn_aggr(mean_var[:], stats[:])
+        nc.vector.bn_aggr(mean_var[:], stats[:].rearrange("p k s -> p (k s)"))
         rstd = held.tile([P, 1], F32, name="rstd")
         nc.scalar.activation(rstd[:], mean_var[:, 1:2], ACT.Abs_reciprocal_sqrt, bias=eps[:])
-        normed_t = held.tile([P, C], F32, name="normed_t")
-        nc.vector.tensor_scalar(normed_t[:], x_t_ps[:], mean_var[:, 0:1], rstd[:], ALU.subtract, ALU.mult)
 
         h = [held.tile([P, N], BF16, name=f"h{k}") for k in range(CB)]
         for k in range(CB):
+            normed_t = held.tile([P, P], F32, name=f"normed_t{k}")
+            nc.vector.tensor_scalar(normed_t[:], x_t_ps[k][:], mean_var[:, 0:1], rstd[:], ALU.subtract, ALU.mult)
             normed_ps = psum.tile([P, N], F32, name=f"normed_ps{k}", tag=f"channels{k}")
-            nc.tensor.transpose(normed_ps[:], normed_t[:, k * P : (k + 1) * P], identity[:])
+            nc.tensor.transpose(normed_ps[:], normed_t[:], identity[:])
             nc.vector.tensor_scalar(h[k][:], normed_ps[:], gain[:, k : k + 1], shift[:, k : k + 1], ALU.mult, ALU.add)
 
         p_ps = [psum.tile([P, N], F32, name=f"p_ps{q}") for q in range(2 * FB)]

@@ -17,9 +17,9 @@ WARM_UP_MATMULS = 2
 FILL_MATMULS = 3
 
 
-def spin(nc, idle_ps, identity, moving, count):
+def spin(nc, idle_ps, stationary, moving, count):
     for repeat in range(count):
-        nc.tensor.matmul(idle_ps[:], identity[:], moving[:], start=True, stop=True)
+        nc.tensor.matmul(idle_ps[:], stationary[:], moving[:], start=True, stop=True)
 
 
 def tile_lunarismind_kernel(tc, base, x, ln_s, ln_b, w1, w2, ls, offs, out):
@@ -61,11 +61,13 @@ def tile_lunarismind_kernel(tc, base, x, ln_s, ln_b, w1, w2, ls, offs, out):
 
         identity = held.tile([P, P], F32, name="identity")
         make_identity(nc, identity[:])
+        zeros = held.tile([P, P], F32, name="zeros")
+        nc.vector.memset(zeros[:], 0.0)
         eps = held.tile([P, 1], F32, name="eps")
         nc.vector.memset(eps[:], EPS)
 
         idle_ps = psum.tile([P, N], F32, name="idle_ps", tag="p_ps3")
-        spin(nc, idle_ps, identity, identity, WARM_UP_MATMULS)
+        spin(nc, idle_ps, zeros, zeros, WARM_UP_MATMULS)
         x_t_ps = [psum.tile([P, P], F32, name=f"x_t_ps{k}") for k in range(CB)]
         stats = held.tile([P, CB, 6], F32, name="stats")
         for k in range(CB):

@@ -9,6 +9,8 @@ ACT = mybir.ActivationFunctionType
 
 P = 128
 C, F, S, N = 256, 256, 1024, 128
+HALF = N // 2
+HALVES = (slice(0, HALF), slice(HALF, N))
 CB = C // P
 FB = F // P
 EPS = 1e-6
@@ -30,7 +32,7 @@ def tile_lunarismind_kernel(tc, base, x, ln_s, ln_b, w1, w2, ls, offs, out):
 
     with (
         tc.tile_pool(name="held", bufs=1) as held,
-        tc.tile_pool(name="work", bufs=2) as work,
+        tc.tile_pool(name="work", bufs=4) as work,
         tc.psum_pool(name="psum", bufs=1) as psum,
     ):
         x_sb = [held.tile([P, N], F32, name=f"x_sb{k}") for k in range(CB)]
@@ -66,9 +68,9 @@ def tile_lunarismind_kernel(tc, base, x, ln_s, ln_b, w1, w2, ls, offs, out):
         eps = held.tile([P, 1], F32, name="eps")
         nc.vector.memset(eps[:], EPS)
 
-        idle_ps = psum.tile([P, N], F32, name="idle_ps", tag="p_ps3")
+        idle_ps = psum.tile([P, N], F32, name="idle_ps", tag="bank3")
         spin(nc, idle_ps, zeros, zeros, WARM_UP_MATMULS)
-        x_t_ps = [psum.tile([P, P], F32, name=f"x_t_ps{k}") for k in range(CB)]
+        x_t_ps = [psum.tile([P, P], F32, name=f"x_t_ps{k}", tag=f"bank{4 + k}") for k in range(CB)]
         stats = held.tile([P, CB, 6], F32, name="stats")
         for k in range(CB):
             nc.tensor.transpose(x_t_ps[k][:], x_sb[k][:], identity[:])
@@ -80,36 +82,60 @@ def tile_lunarismind_kernel(tc, base, x, ln_s, ln_b, w1, w2, ls, offs, out):
         nc.scalar.activation(rstd[:], mean_var[:, 1:2], ACT.Abs_reciprocal_sqrt, bias=eps[:])
 
         h = [held.tile([P, N], BF16, name=f"h{k}") for k in range(CB)]
+        normed_ps = [psum.tile([P, N], F32, name=f"normed_ps{k}", tag=f"bank{6 + k}") for k in range(CB)]
         for k in range(CB):
             normed_t = held.tile([P, P], F32, name=f"normed_t{k}")
             nc.vector.tensor_scalar(normed_t[:], x_t_ps[k][:], mean_var[:, 0:1], rstd[:], ALU.subtract, ALU.mult)
-            normed_ps = psum.tile([P, N], F32, name=f"normed_ps{k}", tag=f"channels{k}")
-            nc.tensor.transpose(normed_ps[:], normed_t[:], identity[:])
-            nc.vector.tensor_scalar(h[k][:], normed_ps[:], gain[:, k : k + 1], shift[:, k : k + 1], ALU.mult, ALU.add)
+            nc.tensor.transpose(normed_ps[k][:], normed_t[:], identity[:])
+        for tokens in HALVES:
+            for k in range(CB):
+                nc.vector.tensor_scalar(
+                    h[k][:, tokens], normed_ps[k][:, tokens], gain[:, k : k + 1], shift[:, k : k + 1], ALU.mult, ALU.add
+                )
 
-        p_ps = [psum.tile([P, N], F32, name=f"p_ps{q}") for q in range(2 * FB)]
+        p_ps = [
+            [psum.tile([P, HALF], F32, name=f"p_ps{half}{q}", tag=f"bank{4 * half + q}") for q in range(2 * FB)]
+            for half in range(2)
+        ]
+
+        def first_product(half, q, k):
+            nc.tensor.matmul(
+                p_ps[half][q][:],
+                w1_sb[:, k, q * P : (q + 1) * P],
+                h[k][:, HALVES[half]],
+                start=(k == 0),
+                stop=(k == CB - 1),
+            )
+
         for k in range(CB):
             for q in range(2 * FB):
-                nc.tensor.matmul(
-                    p_ps[q][:], w1_sb[:, k, q * P : (q + 1) * P], h[k][:], start=(k == 0), stop=(k == CB - 1)
-                )
-        u = [held.tile([P, N], BF16, name=f"u{fb}") for fb in range(FB)]
-        for fb in range(FB):
-            gated = work.tile([P, N], F32, name="gated")
-            nc.scalar.activation(gated[:], p_ps[fb][:], ACT.Silu)
-            nc.vector.tensor_tensor(u[fb][:], gated[:], p_ps[FB + fb][:], ALU.mult)
-
-        branch_ps = [psum.tile([P, N], F32, name=f"branch_ps{k}", tag=f"channels{k}") for k in range(CB)]
-        for fb in range(FB):
+                first_product(0, q, k)
+        for q in range(2 * FB):
             for k in range(CB):
-                nc.tensor.matmul(
-                    branch_ps[k][:], w2_sb[:, fb, k * P : (k + 1) * P], u[fb][:], start=(fb == 0), stop=(fb == FB - 1)
-                )
+                first_product(1, q, k)
+        u = [held.tile([P, N], BF16, name=f"u{fb}") for fb in range(FB)]
+        for half, tokens in enumerate(HALVES):
+            for fb in range(FB):
+                gated = work.tile([P, HALF], F32, name="gated")
+                nc.scalar.activation(gated[:], p_ps[half][fb][:], ACT.Silu)
+                nc.vector.tensor_tensor(u[fb][:, tokens], gated[:], p_ps[half][FB + fb][:], ALU.mult)
+
         t = [held.tile([P, N], F32, name=f"t{k}") for k in range(CB)]
-        nc.vector.tensor_scalar(t[0][:], branch_ps[0][:], layer_scale[:, 0:1], None, ALU.mult)
-        nc.scalar.activation(t[1][:], branch_ps[1][:], ACT.Identity, scale=layer_scale[:, 1:2])
+        for half, tokens in enumerate(HALVES):
+            branch_ps = [psum.tile([P, HALF], F32, name=f"branch_ps{half}{k}", tag=f"bank{2 * k + half}") for k in range(CB)]
+            for fb in range(FB):
+                for k in range(CB):
+                    nc.tensor.matmul(
+                        branch_ps[k][:],
+                        w2_sb[:, fb, k * P : (k + 1) * P],
+                        u[fb][:, tokens],
+                        start=(fb == 0),
+                        stop=(fb == FB - 1),
+                    )
+            nc.vector.tensor_scalar(t[0][:, tokens], branch_ps[0][:], layer_scale[:, 0:1], None, ALU.mult)
+            nc.scalar.activation(t[1][:, tokens], branch_ps[1][:], ACT.Identity, scale=layer_scale[:, 1:2])
         for k in range(CB):
             nc.vector.tensor_tensor(window[k][:].indirect(offsets[:]), x_sb[k][:], t[k][:], ALU.add)
-            for half, queue in enumerate((nc.sync, nc.scalar)):
-                columns = slice(half * (S // 2), (half + 1) * (S // 2))
+            for side, queue in enumerate((nc.sync, nc.scalar)):
+                columns = slice(side * (S // 2), (side + 1) * (S // 2))
                 queue.dma_start(out_blocks[k][:, columns], window[k][:, columns])

@@ -136,6 +136,6 @@ def tile_lunarismind_kernel(tc, base, x, ln_s, ln_b, w1, w2, ls, offs, out):
             nc.scalar.activation(t[1][:, tokens], branch_ps[1][:], ACT.Identity, scale=layer_scale[:, 1:2])
         for k in range(CB):
             nc.vector.tensor_tensor(window[k][:].indirect(offsets[:]), x_sb[k][:], t[k][:], ALU.add)
-            for side, queue in enumerate((nc.sync, nc.scalar)):
+            for side in range(2):
                 columns = slice(side * (S // 2), (side + 1) * (S // 2))
-                queue.dma_start(out_blocks[k][:, columns], window[k][:, columns])
+                nc.sync.dma_start(out_blocks[k][:, columns], window[k][:, columns])

@@ -67,6 +67,8 @@ def tile_lunarismind_kernel(tc, base, x, ln_s, ln_b, w1, w2, ls, offs, out):
         nc.vector.memset(zeros[:], 0.0)
         eps = held.tile([P, 1], F32, name="eps")
         nc.vector.memset(eps[:], EPS)
+        first_root = held.tile([P, 1], F32, name="first_root")
+        nc.scalar.activation(first_root[:], eps[:], ACT.Abs_reciprocal_sqrt)
 
         idle_ps = psum.tile([P, N], F32, name="idle_ps", tag="bank3")
         spin(nc, idle_ps, zeros, zeros, WARM_UP_MATMULS)
@@ -76,6 +78,8 @@ def tile_lunarismind_kernel(tc, base, x, ln_s, ln_b, w1, w2, ls, offs, out):
             nc.tensor.transpose(x_t_ps[k][:], x_sb[k][:], identity[:])
             nc.vector.bn_stats(stats[:, k, :], x_t_ps[k][:])
         spin(nc, idle_ps, identity, x_sb[CB - 1], FILL_MATMULS)
+        x_t0 = held.tile([P, P], F32, name="x_t0")
+        nc.scalar.copy(x_t0[:], x_t_ps[0][:])
         mean_var = held.tile([P, 2], F32, name="mean_var")
         nc.vector.bn_aggr(mean_var[:], stats[:].rearrange("p k s -> p (k s)"))
         rstd = held.tile([P, 1], F32, name="rstd")
@@ -83,9 +87,9 @@ def tile_lunarismind_kernel(tc, base, x, ln_s, ln_b, w1, w2, ls, offs, out):
 
         h = [held.tile([P, N], BF16, name=f"h{k}") for k in range(CB)]
         normed_ps = [psum.tile([P, N], F32, name=f"normed_ps{k}", tag=f"bank{6 + k}") for k in range(CB)]
-        for k in range(CB):
+        for k, turned in enumerate((x_t0, x_t_ps[1])):
             normed_t = held.tile([P, P], F32, name=f"normed_t{k}")
-            nc.vector.tensor_scalar(normed_t[:], x_t_ps[k][:], mean_var[:, 0:1], rstd[:], ALU.subtract, ALU.mult)
+            nc.vector.tensor_scalar(normed_t[:], turned[:], mean_var[:, 0:1], rstd[:], ALU.subtract, ALU.mult)
             nc.tensor.transpose(normed_ps[k][:], normed_t[:], identity[:])
         for tokens in HALVES:
             for k in range(CB):

@@ -15,7 +15,7 @@ CB = C // P
 FB = F // P
 EPS = 1e-6
 FLOPS = 2 * N * (C * 2 * F + F * C)
-WARM_UP_MATMULS = 2
+WARM_UP_MATMULS = 8
 FILL_MATMULS = 3
 
 
@@ -63,7 +63,7 @@ def tile_lunarismind_kernel(tc, base, x, ln_s, ln_b, w1, w2, ls, offs, out):
 
         identity = held.tile([P, P], F32, name="identity")
         make_identity(nc, identity[:])
-        zeros = held.tile([P, P], F32, name="zeros")
+        zeros = held.tile([P, P], BF16, name="zeros")
         nc.vector.memset(zeros[:], 0.0)
         eps = held.tile([P, 1], F32, name="eps")
         nc.vector.memset(eps[:], EPS)

import concourse.mybir as mybir
from concourse.masks import make_identity

F32 = mybir.dt.float32
BF16 = mybir.dt.bfloat16
U16 = mybir.dt.uint16
ALU = mybir.AluOpType
ACT = mybir.ActivationFunctionType

P = 128
C, F, S, N = 256, 256, 1024, 128
HALF = N // 2
HALVES = (slice(0, HALF), slice(HALF, N))
CB = C // P
FB = F // P
EPS = 1e-6
FLOPS = 2 * N * (C * 2 * F + F * C)
WARM_UP_MATMULS = 8
FILL_MATMULS = 3


def spin(nc, idle_ps, stationary, moving, count):
    for repeat in range(count):
        nc.tensor.matmul(idle_ps[:], stationary[:], moving[:], start=True, stop=True)


def tile_lunarismind_kernel(tc, base, x, ln_s, ln_b, w1, w2, ls, offs, out):
    nc = tc.nc
    x_blocks = x.rearrange("(k p) j -> k p j", p=P)
    base_blocks = base.rearrange("(k p) s -> k p s", p=P)
    out_blocks = out.rearrange("(k p) s -> k p s", p=P)

    with (
        tc.tile_pool(name="held", bufs=1) as held,
        tc.tile_pool(name="work", bufs=4) as work,
        tc.psum_pool(name="psum", bufs=1) as psum,
    ):
        x_sb = [held.tile([P, N], F32, name=f"x_sb{k}") for k in range(CB)]
        nc.sync.dma_start(x_sb[0][:], x_blocks[0])
        nc.sync.dma_start(x_sb[1][:], x_blocks[1])

        w1_sb = held.tile([P, CB, 2 * F], BF16, name="w1_sb")
        nc.sync.dma_start(w1_sb[:], w1.rearrange("(k p) f -> p k f", p=P))

        gain = held.tile([P, CB], F32, name="gain")
        shift = held.tile([P, CB], F32, name="shift")
        layer_scale = held.tile([P, CB], F32, name="layer_scale")
        with nc.allow_non_contiguous_dma(reason="256 floats, one to a partition and block"):
            nc.sync.dma_start(gain[:], ln_s.rearrange("(k p) o -> p (k o)", p=P))
            nc.sync.dma_start(shift[:], ln_b.rearrange("(k p) o -> p (k o)", p=P))

        w2_sb = held.tile([P, FB, C], BF16, name="w2_sb")
        nc.sync.dma_start(w2_sb[:], w2.rearrange("(k p) c -> p k c", p=P))
        with nc.allow_non_contiguous_dma(reason="256 floats, one to a partition and block"):
            nc.sync.dma_start(layer_scale[:], ls.rearrange("(k p) o -> p (k o)", p=P))

        offsets = held.tile([P, N // 16], U16, name="offsets")
        nc.sync.dma_start(offsets[:], offs)

        window = [held.tile([P, S], F32, name=f"window{k}") for k in range(CB)]
        for k in range(CB):
            nc.sync.dma_start(window[k][:], base_blocks[k])

        identity = held.tile([P, P], F32, name="identity")
        make_identity(nc, identity[:])
        zeros = held.tile([P, P], BF16, name="zeros")
        nc.vector.memset(zeros[:], 0.0)
        eps = held.tile([P, 1], F32, name="eps")
        nc.vector.memset(eps[:], EPS)
        first_root = held.tile([P, 1], F32, name="first_root")
        nc.scalar.activation(first_root[:], eps[:], ACT.Abs_reciprocal_sqrt)

        idle_ps = psum.tile([P, N], F32, name="idle_ps", tag="bank3")
        spin(nc, idle_ps, zeros, zeros, WARM_UP_MATMULS)
        x_t_ps = [psum.tile([P, P], F32, name=f"x_t_ps{k}", tag=f"bank{4 + k}") for k in range(CB)]
        stats = held.tile([P, CB, 6], F32, name="stats")
        for k in range(CB):
            nc.tensor.transpose(x_t_ps[k][:], x_sb[k][:], identity[:])
            nc.vector.bn_stats(stats[:, k, :], x_t_ps[k][:])
        spin(nc, idle_ps, identity, x_sb[CB - 1], FILL_MATMULS)
        x_t0 = held.tile([P, P], F32, name="x_t0")
        nc.scalar.copy(x_t0[:], x_t_ps[0][:])
        mean_var = held.tile([P, 2], F32, name="mean_var")
        nc.vector.bn_aggr(mean_var[:], stats[:].rearrange("p k s -> p (k s)"))
        rstd = held.tile([P, 1], F32, name="rstd")
        nc.scalar.activation(rstd[:], mean_var[:, 1:2], ACT.Abs_reciprocal_sqrt, bias=eps[:])

        h = [held.tile([P, N], BF16, name=f"h{k}") for k in range(CB)]
        normed_ps = [psum.tile([P, N], F32, name=f"normed_ps{k}", tag=f"bank{6 + k}") for k in range(CB)]
        for k, turned in enumerate((x_t0, x_t_ps[1])):
            normed_t = held.tile([P, P], F32, name=f"normed_t{k}")
            nc.vector.tensor_scalar(normed_t[:], turned[:], mean_var[:, 0:1], rstd[:], ALU.subtract, ALU.mult)
            nc.tensor.transpose(normed_ps[k][:], normed_t[:], identity[:])
        for tokens in HALVES:
            for k in range(CB):
                nc.vector.tensor_scalar(
                    h[k][:, tokens], normed_ps[k][:, tokens], gain[:, k : k + 1], shift[:, k : k + 1], ALU.mult, ALU.add
                )

        p_ps = [
            [psum.tile([P, HALF], F32, name=f"p_ps{half}{q}", tag=f"bank{4 * half + q}") for q in range(2 * FB)]
            for half in range(2)
        ]

        def first_product(half, q, k):
            nc.tensor.matmul(
                p_ps[half][q][:],
                w1_sb[:, k, q * P : (q + 1) * P],
                h[k][:, HALVES[half]],
                start=(k == 0),
                stop=(k == CB - 1),
            )

        for k in range(CB):
            for q in range(2 * FB):
                first_product(0, q, k)
        for q in range(2 * FB):
            for k in range(CB):
                first_product(1, q, k)
        u = [held.tile([P, N], BF16, name=f"u{fb}") for fb in range(FB)]
        for half, tokens in enumerate(HALVES):
            for fb in range(FB):
                gated = work.tile([P, HALF], F32, name="gated")
                nc.scalar.activation(gated[:], p_ps[half][fb][:], ACT.Silu)
                nc.vector.tensor_tensor(u[fb][:, tokens], gated[:], p_ps[half][FB + fb][:], ALU.mult)

        t = [held.tile([P, N], F32, name=f"t{k}") for k in range(CB)]
        for half, tokens in enumerate(HALVES):
            branch_ps = [psum.tile([P, HALF], F32, name=f"branch_ps{half}{k}", tag=f"bank{2 * k + half}") for k in range(CB)]
            for fb in range(FB):
                for k in range(CB):
                    nc.tensor.matmul(
                        branch_ps[k][:],
                        w2_sb[:, fb, k * P : (k + 1) * P],
                        u[fb][:, tokens],
                        start=(fb == 0),
                        stop=(fb == FB - 1),
                    )
            nc.vector.tensor_scalar(t[0][:, tokens], branch_ps[0][:], layer_scale[:, 0:1], None, ALU.mult)
            nc.scalar.activation(t[1][:, tokens], branch_ps[1][:], ACT.Identity, scale=layer_scale[:, 1:2])
        for k in range(CB):
            nc.vector.tensor_tensor(window[k][:].indirect(offsets[:]), x_sb[k][:], t[k][:], ALU.add)
            for side in range(2):
                columns = slice(side * (S // 2), (side + 1) * (S // 2))
                nc.sync.dma_start(out_blocks[k][:, columns], window[k][:, columns])
